import numpy as np
import ml_dtypes


def mxq(x, axis, fmt="e4m3"):
    dtype, down = {"e4m3": (ml_dtypes.float8_e4m3fn, 7), "e5m2": (ml_dtypes.float8_e5m2, 14)}[fmt]
    v = np.moveaxis(np.asarray(x, np.float32).astype(ml_dtypes.bfloat16).astype(np.float64), axis, -1)
    blocks = v.reshape(v.shape[:-1] + (-1, 32))
    amax = np.abs(blocks).max(-1, keepdims=True)
    byte = np.maximum(np.where(amax > 0, np.frexp(amax)[1] - 1 + 127, 0) - down, 1)
    scale = np.exp2(byte - 127.0)
    codes = (blocks / scale).astype(np.float32).astype(dtype).astype(np.float64)
    return np.moveaxis((codes * scale).reshape(v.shape), -1, axis)


WIDE = False


def mx_kscale(k):
    if not WIDE:
        return np.ones(k)
    levels = np.array([10, -10, 5, -5, 0])
    a = np.random.permutation(np.resize(levels, k // 512 * 4)).reshape(k // 512, 4)
    idx = np.arange(k)
    return np.exp2(a[idx // 512, idx % 128 // 32])


BF16 = ml_dtypes.bfloat16


def bf(x):
    return np.asarray(x, np.float32).astype(BF16)


def f64(x):
    return np.asarray(x).astype(np.float64)


N, IN_DIM, HID, NUM_CLASSES, AVG_DEG = 2048, 512, 512, 512, 32


def sigmoid(v):
    return 1.0 / (1.0 + np.exp(-v))


def setup_inputs():
    t = mx_kscale(HID)
    edges = np.random.uniform(size=(N, N)) < AVG_DEG / N
    return {"A": bf(edges * (0.5 + np.random.uniform(size=(N, N)))),
            "deg_inv_sqrt": bf(1.0 / np.sqrt(1.0 + AVG_DEG * (0.75 + 0.5 * np.random.uniform(size=N)))),
            "h1": bf(np.maximum(np.random.standard_normal((N, HID)) * 2.0 / np.sqrt(AVG_DEG), 0.0) * t),
            "W2": bf(np.random.standard_normal((HID, NUM_CLASSES)) * 4.0 / np.sqrt(HID) / t[:, None]),
            "b2": bf(np.random.standard_normal(NUM_CLASSES) * 0.1),
            "x": bf(np.random.standard_normal((N, NUM_CLASSES)) * 0.5),
            "sigmoid_param": bf(4.0 + 0.4 * np.random.standard_normal(1))}


def reference(A, deg_inv_sqrt, h1, W2, b2, x, sigmoid_param):
    dis = f64(deg_inv_sqrt)[:, None]
    g = mxq(f64(h1), 1, "e4m3") @ mxq(f64(W2), 0, "e4m3")
    m = dis * g
    agg = mxq(f64(A), 0, "e4m3").T @ mxq(m, 0, "e4m3")
    h = dis * agg + dis ** 2 * g + f64(b2)
    return sigmoid(f64(sigmoid_param) * (h + f64(x)))

@@ -1,0 +1,334 @@
+from contextlib import ExitStack
+
+import concourse.mybir as mybir
+from concourse.masks import make_identity
+
+F32 = mybir.dt.float32
+BF16 = mybir.dt.bfloat16
+U32 = mybir.dt.uint32
+U8 = mybir.dt.uint8
+FP8X4 = mybir.dt.float8_e4m3fn_x4
+ACT = mybir.ActivationFunctionType
+ALU = mybir.AluOpType
+
+P = 128
+PACK = 4
+K_PASS = P * PACK
+NODES = 2048
+HID = 512
+CLS = 512
+TILES = NODES // P
+CHUNKS = NODES // K_PASS
+SUB = 512
+SUB_TILES = SUB // P
+ROUNDS = NODES // SUB
+SUBS = ROUNDS * CHUNKS
+VEC_COLS = 176
+
+FLOPS = 2 * NODES * HID * CLS + 2 * NODES * NODES * CLS
+
+
+def interleave(dst, src):
+    return (
+        dst.rearrange("p (c i) t -> p c t i", i=4),
+        src.rearrange("p t (c i) -> p c t i", i=4),
+    )
+
+
+def tile_gcnnodeclassifiernetwork_pb_kernel(
+    tc, A, deg_inv_sqrt, h1, W2, b2, x, sigmoid_param, out
+):
+    nc = tc.nc
+    with ExitStack() as ctx:
+        const = ctx.enter_context(tc.tile_pool(name="const", bufs=1))
+        keep = ctx.enter_context(tc.tile_pool(name="keep", bufs=1))
+        h1_pool = ctx.enter_context(tc.tile_pool(name="h1_pool", bufs=2))
+        raw_pool = ctx.enter_context(tc.tile_pool(name="raw_pool", bufs=8))
+        grp_pool = ctx.enter_context(tc.tile_pool(name="grp_pool", bufs=6))
+        mid_pool = ctx.enter_context(tc.tile_pool(name="mid_pool", bufs=2))
+        res_pool = ctx.enter_context(tc.tile_pool(name="res_pool", bufs=8))
+        psum = ctx.enter_context(tc.psum_pool(name="psum", bufs=8))
+        ctx.enter_context(tc.manual_schedule())
+
+        w_codes = keep.tile([P, CLS], U32, name="w_codes", align_bytes=64)
+        w_scales = keep.tile([P, CLS], U8, name="w_scales", align_bytes=64)
+        h_codes = keep.tile([P, NODES], U32, name="h_codes", align_bytes=64)
+        h_scales = keep.tile([P, NODES], U8, name="h_scales", align_bytes=64)
+        m_codes = keep.tile([P, CHUNKS, CLS], U32, name="m_codes", align_bytes=64)
+        m_scales = keep.tile([P, CHUNKS, CLS], U8, name="m_scales", align_bytes=64)
+        a_codes = keep.tile([P, CHUNKS, NODES], U32, name="a_codes", align_bytes=64)
+        a_scales = keep.tile([P, CHUNKS, NODES], U8, name="a_scales", align_bytes=64)
+        y = keep.tile([P, TILES, CLS], F32, name="y")
+        x_sb = keep.tile([P, TILES, CLS], BF16, name="x_sb")
+        d_col = const.tile([P, TILES], F32, name="d_col")
+        slope = const.tile([P, 1], F32, name="slope")
+        ident_f32 = const.tile([P, P], F32, name="ident_f32")
+        ident_bf = const.tile([P, P], BF16, name="ident_bf")
+        ones = const.tile([P, P], BF16, name="ones")
+        w_raw = raw_pool.tile([P, PACK, CLS], BF16, name="w_raw", tag="a_raw")
+        d_rows = const.tile([P, P], BF16, name="d_rows")
+        b2_rows = const.tile([P, CLS], BF16, name="b2_rows")
+        slope_bf = const.tile([P, 1], BF16, name="slope_bf")
+
+        h1_tiles = {}
+        a_tiles = {}
+        h_grps = {}
+        u_tiles = {}
+        m_grps = {}
+        a_grps = {}
+        acc = {}
+        xb_tiles = {}
+
+        def load_small():
+            nc.vector.memset(d_rows[:], 0.0)
+            nc.scalar.dma_start(
+                out=d_rows[0:TILES, :], in_=deg_inv_sqrt.rearrange("(t p) -> t p", p=P)
+            )
+            nc.vector.memset(b2_rows[:], 0.0)
+            nc.vector.memset(ones[:], 1.0)
+            nc.scalar.dma_start(out=b2_rows[0:1, :], in_=b2.unsqueeze(0))
+            nc.scalar.dma_start(out=slope_bf[:], in_=sigmoid_param.partition_broadcast(P))
+
+        def load_w2():
+            for u in range(2):
+                nc.sync.dma_start(
+                    out=w_raw[:, 2 * u : 2 * u + 2, :],
+                    in_=W2[u * 256 : (u + 1) * 256, :].rearrange("(q e) c -> q e c", e=2),
+                )
+
+        def load_h1(c):
+            h1_sb = h1_pool.tile([P, PACK, HID], BF16, name="h1_sb")
+            nc.sync.dma_start(
+                out=h1_sb[:],
+                in_=h1[c * K_PASS : (c + 1) * K_PASS, :].rearrange("(t p) k -> p t k", p=P),
+            )
+            h1_tiles[c] = h1_sb
+
+        def load_a(k):
+            r, c = divmod(k, CHUNKS)
+            a_raw = raw_pool.tile([P, PACK, SUB], BF16, name="a_raw")
+            nc.sync.dma_start(
+                out=a_raw[:],
+                in_=A[c * K_PASS : (c + 1) * K_PASS, r * SUB : (r + 1) * SUB].rearrange(
+                    "(t p) w -> p t w", p=P
+                ),
+            )
+            a_tiles[k] = a_raw
+
+        def load_x(r):
+            nc.sync.dma_start(
+                out=x_sb[:, r * SUB_TILES : (r + 1) * SUB_TILES, :],
+                in_=x[r * SUB : (r + 1) * SUB, :].rearrange("(t p) c -> p t c", p=P),
+            )
+
+        def warm_sigmoid():
+            warm = const.tile([P, 1], F32, name="warm")
+            nc.vector.memset(warm[:], 0.0)
+            warm_out = const.tile([P, 1], F32, name="warm_out")
+            nc.scalar.activation(out=warm_out[:], in_=warm[:], func=ACT.Sigmoid)
+
+        def spread_small():
+            nc.vector.tensor_copy(out=ident_bf[:], in_=ident_f32[:])
+            d_ps = psum.tile([P, P], BF16, name="d_ps", tag="bank")
+            nc.tensor.transpose(d_ps[:], d_rows[:], ident_bf[:])
+            nc.vector.tensor_copy(out=d_col[:], in_=d_ps[:, 0:TILES])
+            nc.vector.tensor_copy(out=slope[:], in_=slope_bf[:])
+
+        w_grp = grp_pool.tile([P, CLS, PACK], BF16, name="w_grp", tag="a_grp", align_bytes=64)
+
+        def regroup_w2():
+            w_dst, w_src = interleave(w_grp[:], w_raw[:])
+            nc.vector.tensor_copy(out=w_dst, in_=w_src)
+
+        def quantise_w2():
+            nc.vector.quantize_mx(
+                out=w_codes[:].bitcast(FP8X4),
+                scales=w_scales[:],
+                in_=w_grp[:].rearrange("p c t -> p (c t)"),
+            )
+
+        def transpose_h1(c):
+            h1_words = h1_tiles[c][:].bitcast(F32)
+            h_grp = mid_pool.tile([P, K_PASS, PACK], BF16, name="h_grp", align_bytes=64)
+            h_grp_words = h_grp[:].bitcast(F32)
+            for pair in range(2):
+                xt = psum.tile([P, 2, 2, P], F32, name="xt", tag="bank")
+                for s in range(2):
+                    for u in range(2):
+                        nc.tensor.transpose(
+                            xt[:, s, u, :],
+                            h1_words[:, 2 * pair + s, u * P : (u + 1) * P],
+                            ident_f32[:],
+                        )
+                nc.scalar.copy(
+                    out=h_grp_words[:, pair * 2 * P : (pair + 1) * 2 * P, :].rearrange(
+                        "p (s r) u -> p s r u", s=2
+                    ),
+                    in_=xt[:].rearrange("p s u r -> p s r u"),
+                )
+            h_grps[c] = h_grp
+
+        def quantise_h1(c):
+            cols = slice(c * K_PASS, (c + 1) * K_PASS)
+            nc.vector.quantize_mx(
+                out=h_codes[:, cols].bitcast(FP8X4),
+                scales=h_scales[:, cols],
+                in_=h_grps[c][:].rearrange("p r t -> p (r t)"),
+            )
+
+        def first_matmul(c):
+            u_sb = mid_pool.tile([P, PACK, CLS], F32, name="u_sb")
+            for t in range(PACK):
+                n = c * PACK + t
+                cols = slice(n * P, (n + 1) * P)
+                g_ps = psum.tile([P, CLS], F32, name="g_ps", tag="bank")
+                nc.tensor.matmul_mx(
+                    out=g_ps[:],
+                    lhsT=h_codes[:, cols].bitcast(FP8X4),
+                    lhsT_scale=h_scales[:, cols],
+                    rhs=w_codes[:].bitcast(FP8X4),
+                    rhs_scale=w_scales[:],
+                    start=True,
+                    stop=True,
+                )
+                nc.scalar.activation(
+                    out=u_sb[:, t, :], in_=g_ps[:], func=ACT.Copy, scale=d_col[:, n : n + 1]
+                )
+            u_tiles[c] = u_sb
+
+        def skip_and_bias(c):
+            for t in range(PACK):
+                n = c * PACK + t
+                xb_ps = psum.tile([P, CLS], F32, name="xb_ps", tag="bank")
+                nc.tensor.matmul(xb_ps[:], lhsT=ident_bf[:], rhs=x_sb[:, n, :], start=True, stop=False)
+                nc.tensor.matmul(xb_ps[:], lhsT=ones[:], rhs=b2_rows[:], start=False, stop=True)
+                xb_tiles[n] = xb_ps
+
+        def self_loop(c):
+            for t in range(PACK):
+                n = c * PACK + t
+                nc.vector.scalar_tensor_tensor(
+                    out=y[:, n, :],
+                    in0=u_tiles[c][:, t, :],
+                    scalar=d_col[:, n : n + 1],
+                    in1=xb_tiles[n][:],
+                    op0=ALU.mult,
+                    op1=ALU.add,
+                )
+
+        def regroup_m(c):
+            m_grp = mid_pool.tile([P, CLS, PACK], BF16, name="m_grp", align_bytes=64)
+            m_dst, m_src = interleave(m_grp[:], u_tiles[c][:])
+            nc.vector.tensor_copy(out=m_dst, in_=m_src)
+            m_grps[c] = m_grp
+
+        def quantise_m(c):
+            nc.vector.quantize_mx(
+                out=m_codes[:, c, :].bitcast(FP8X4),
+                scales=m_scales[:, c, :],
+                in_=m_grps[c][:].rearrange("p w t -> p (w t)"),
+            )
+
+        def regroup_a(k):
+            a_raw = a_tiles[k]
+            a_grp = grp_pool.tile([P, SUB, PACK], BF16, name="a_grp", align_bytes=64)
+            s_dst, s_src = interleave(a_grp[:, VEC_COLS:SUB, :], a_raw[:, :, VEC_COLS:SUB])
+            nc.scalar.copy(out=s_dst, in_=s_src)
+            v_dst, v_src = interleave(a_grp[:, 0:VEC_COLS, :], a_raw[:, :, 0:VEC_COLS])
+            nc.vector.tensor_copy(out=v_dst, in_=v_src)
+            a_grps[k] = a_grp
+
+        def quantise_a(k):
+            r, c = divmod(k, CHUNKS)
+            cols = slice(r * SUB, (r + 1) * SUB)
+            nc.vector.quantize_mx(
+                out=a_codes[:, c, cols].bitcast(FP8X4),
+                scales=a_scales[:, c, cols],
+                in_=a_grps[k][:].rearrange("p w t -> p (w t)"),
+            )
+
+        def second_matmul(k):
+            r, c = divmod(k, CHUNKS)
+            for j in range(SUB_TILES):
+                jt = r * SUB_TILES + j
+                if c == 0:
+                    acc[jt] = psum.tile([P, CLS], F32, name="acc", tag="bank")
+                cols = slice(jt * P, (jt + 1) * P)
+                nc.tensor.matmul_mx(
+                    out=acc[jt][:],
+                    lhsT=a_codes[:, c, cols].bitcast(FP8X4),
+                    lhsT_scale=a_scales[:, c, cols],
+                    rhs=m_codes[:, c, :].bitcast(FP8X4),
+                    rhs_scale=m_scales[:, c, :],
+                    start=(c == 0),
+                    stop=(c == CHUNKS - 1),
+                )
+
+        def finish(jt):
+            res = res_pool.tile([P, CLS], F32, name="res")
+            nc.vector.scalar_tensor_tensor(
+                out=res[:],
+                in0=acc[jt][:],
+                scalar=d_col[:, jt : jt + 1],
+                in1=y[:, jt, :],
+                op0=ALU.mult,
+                op1=ALU.add,
+            )
+            nc.scalar.activation(out=res[:], in_=res[:], func=ACT.Sigmoid, scale=slope[:, 0:1])
+            nc.sync.dma_start(out=out[jt * P : (jt + 1) * P, :], in_=res[:])
+
+        load_small()
+        load_h1(0)
+        load_w2()
+        load_a(0)
+        load_x(0)
+        load_h1(1)
+        load_a(1)
+        load_a(2)
+        warm_sigmoid()
+        make_identity(nc, ident_f32[:])
+        transpose_h1(0)
+        spread_small()
+        regroup_w2()
+        regroup_a(0)
+        quantise_w2()
+        quantise_h1(0)
+        for c in range(CHUNKS):
+            if c + 1 < CHUNKS:
+                load_x(c + 1)
+            if c + 2 < CHUNKS:
+                load_h1(c + 2)
+            load_a(2 * c + 3)
+            load_a(2 * c + 4)
+            first_matmul(c)
+            skip_and_bias(c)
+            if c + 1 < CHUNKS:
+                transpose_h1(c + 1)
+            if c > 0:
+                quantise_m(c - 1)
+                quantise_a(2 * c - 1)
+            quantise_a(2 * c)
+            regroup_a(2 * c + 1)
+            regroup_a(2 * c + 2)
+            self_loop(c)
+            if c + 1 < CHUNKS:
+                quantise_h1(c + 1)
+            regroup_m(c)
+        for k in range(2 * CHUNKS + 3, SUBS):
+            load_a(k)
+        quantise_m(CHUNKS - 1)
+        quantise_a(2 * CHUNKS - 1)
+        for c in range(CHUNKS):
+            second_matmul(c)
+            second_matmul(CHUNKS + c)
+        for i in range(8):
+            k = 2 * CHUNKS + i
+            if k + 1 < SUBS:
+                regroup_a(k + 1)
+            quantise_a(k)
+            second_matmul(k)
+            if i >= 1:
+                finish(2 * i - 2)
+                finish(2 * i - 1) if i < 7 else None
+        for jt in range(13, TILES):
+            finish(jt)

@@ -44,7 +44,7 @@ def tile_gcnnodeclassifiernetwork_pb_kernel(
         keep = ctx.enter_context(tc.tile_pool(name="keep", bufs=1))
         h1_pool = ctx.enter_context(tc.tile_pool(name="h1_pool", bufs=2))
         raw_pool = ctx.enter_context(tc.tile_pool(name="raw_pool", bufs=8))
-        grp_pool = ctx.enter_context(tc.tile_pool(name="grp_pool", bufs=6))
+        grp_pool = ctx.enter_context(tc.tile_pool(name="grp_pool", bufs=8))
         mid_pool = ctx.enter_context(tc.tile_pool(name="mid_pool", bufs=2))
         res_pool = ctx.enter_context(tc.tile_pool(name="res_pool", bufs=8))
         psum = ctx.enter_context(tc.psum_pool(name="psum", bufs=8))
@@ -59,7 +59,6 @@ def tile_gcnnodeclassifiernetwork_pb_kernel(
         a_codes = keep.tile([P, CHUNKS, NODES], U32, name="a_codes", align_bytes=64)
         a_scales = keep.tile([P, CHUNKS, NODES], U8, name="a_scales", align_bytes=64)
         y = keep.tile([P, TILES, CLS], F32, name="y")
-        x_sb = keep.tile([P, TILES, CLS], BF16, name="x_sb")
         d_col = const.tile([P, TILES], F32, name="d_col")
         slope = const.tile([P, 1], F32, name="slope")
         ident_f32 = const.tile([P, P], F32, name="ident_f32")
@@ -77,6 +76,7 @@ def tile_gcnnodeclassifiernetwork_pb_kernel(
         m_grps = {}
         a_grps = {}
         acc = {}
+        x_tiles = {}
         xb_tiles = {}
 
         def load_small():
@@ -115,11 +115,13 @@ def tile_gcnnodeclassifiernetwork_pb_kernel(
             )
             a_tiles[k] = a_raw
 
-        def load_x(r):
+        def load_x(c):
+            x_sb = h1_pool.tile([P, PACK, CLS], BF16, name="x_sb")
             nc.sync.dma_start(
-                out=x_sb[:, r * SUB_TILES : (r + 1) * SUB_TILES, :],
-                in_=x[r * SUB : (r + 1) * SUB, :].rearrange("(t p) c -> p t c", p=P),
+                out=x_sb[:],
+                in_=x[c * K_PASS : (c + 1) * K_PASS, :].rearrange("(t p) k -> p t k", p=P),
             )
+            x_tiles[c] = x_sb
 
         def warm_sigmoid():
             warm = const.tile([P, 1], F32, name="warm")
@@ -200,7 +202,7 @@ def tile_gcnnodeclassifiernetwork_pb_kernel(
             for t in range(PACK):
                 n = c * PACK + t
                 xb_ps = psum.tile([P, CLS], F32, name="xb_ps", tag="bank")
-                nc.tensor.matmul(xb_ps[:], lhsT=ident_bf[:], rhs=x_sb[:, n, :], start=True, stop=False)
+                nc.tensor.matmul(xb_ps[:], lhsT=ident_bf[:], rhs=x_tiles[c][:, t, :], start=True, stop=False)
                 nc.tensor.matmul(xb_ps[:], lhsT=ones[:], rhs=b2_rows[:], start=False, stop=True)
                 xb_tiles[n] = xb_ps
 
@@ -277,58 +279,51 @@ def tile_gcnnodeclassifiernetwork_pb_kernel(
             nc.scalar.activation(out=res[:], in_=res[:], func=ACT.Sigmoid, scale=slope[:, 0:1])
             nc.sync.dma_start(out=out[jt * P : (jt + 1) * P, :], in_=res[:])
 
+        LEAD = 6
+        LAG = 5
         load_small()
         load_h1(0)
         load_w2()
-        load_a(0)
-        load_x(0)
         load_h1(1)
-        load_a(1)
-        load_a(2)
+        load_x(0)
+        load_a(0)
+        load_x(1)
         warm_sigmoid()
         make_identity(nc, ident_f32[:])
         transpose_h1(0)
         spread_small()
         regroup_w2()
-        regroup_a(0)
         quantise_w2()
         quantise_h1(0)
         for c in range(CHUNKS):
-            if c + 1 < CHUNKS:
-                load_x(c + 1)
             if c + 2 < CHUNKS:
                 load_h1(c + 2)
-            load_a(2 * c + 3)
-            load_a(2 * c + 4)
-            first_matmul(c)
-            skip_and_bias(c)
+            load_a(c + 1)
+            if c + 2 < CHUNKS:
+                load_x(c + 2)
             if c + 1 < CHUNKS:
                 transpose_h1(c + 1)
+            first_matmul(c)
+            skip_and_bias(c)
             if c > 0:
-                quantise_m(c - 1)
-                quantise_a(2 * c - 1)
-            quantise_a(2 * c)
-            regroup_a(2 * c + 1)
-            regroup_a(2 * c + 2)
-            self_loop(c)
+                regroup_m(c - 1)
             if c + 1 < CHUNKS:
                 quantise_h1(c + 1)
-            regroup_m(c)
-        for k in range(2 * CHUNKS + 3, SUBS):
+            if c > 0:
+                quantise_m(c - 1)
+            self_loop(c)
+            regroup_a(c)
+        for k in range(CHUNKS + 1, SUBS):
             load_a(k)
+        regroup_m(CHUNKS - 1)
         quantise_m(CHUNKS - 1)
-        quantise_a(2 * CHUNKS - 1)
-        for c in range(CHUNKS):
-            second_matmul(c)
-            second_matmul(CHUNKS + c)
-        for i in range(8):
-            k = 2 * CHUNKS + i
-            if k + 1 < SUBS:
-                regroup_a(k + 1)
-            quantise_a(k)
-            second_matmul(k)
-            if i >= 1:
-                finish(2 * i - 2)
-                finish(2 * i - 1) if i < 7 else None
-        for jt in range(13, TILES):
-            finish(jt)
+        for k in range(CHUNKS, LEAD):
+            regroup_a(k)
+        for k in range(SUBS + LAG):
+            if k < SUBS:
+                quantise_a(k)
+                second_matmul(k)
+            if k + LEAD < SUBS:
+                regroup_a(k + LEAD)
+            if k >= LAG:
+                finish(k - LAG)

@@ -19,16 +19,21 @@ HID = 512
 CLS = 512
 TILES = NODES // P
 CHUNKS = NODES // K_PASS
-SUB = 512
-SUB_TILES = SUB // P
-ROUNDS = NODES // SUB
+ROUND = 512
+ROUND_TILES = ROUND // P
+ROUNDS = NODES // ROUND
 SUBS = ROUNDS * CHUNKS
+PSUM_BANKS = 8
+
 VEC_COLS = 176
+LEAD = 6
+LAG = CHUNKS + 1
+assert TILES == SUBS
 
 FLOPS = 2 * NODES * HID * CLS + 2 * NODES * NODES * CLS
 
 
-def interleave(dst, src):
+def side_by_side(dst, src):
     return (
         dst.rearrange("p (c i) t -> p c t i", i=4),
         src.rearrange("p t (c i) -> p c t i", i=4),
@@ -42,12 +47,12 @@ def tile_gcnnodeclassifiernetwork_pb_kernel(
     with ExitStack() as ctx:
         const = ctx.enter_context(tc.tile_pool(name="const", bufs=1))
         keep = ctx.enter_context(tc.tile_pool(name="keep", bufs=1))
-        h1_pool = ctx.enter_context(tc.tile_pool(name="h1_pool", bufs=2))
-        raw_pool = ctx.enter_context(tc.tile_pool(name="raw_pool", bufs=8))
-        grp_pool = ctx.enter_context(tc.tile_pool(name="grp_pool", bufs=8))
+        in_pool = ctx.enter_context(tc.tile_pool(name="in_pool", bufs=2))
+        raw_pool = ctx.enter_context(tc.tile_pool(name="raw_pool", bufs=LEAD + 2))
+        grp_pool = ctx.enter_context(tc.tile_pool(name="grp_pool", bufs=LEAD + 2))
         mid_pool = ctx.enter_context(tc.tile_pool(name="mid_pool", bufs=2))
         res_pool = ctx.enter_context(tc.tile_pool(name="res_pool", bufs=8))
-        psum = ctx.enter_context(tc.psum_pool(name="psum", bufs=8))
+        psum = ctx.enter_context(tc.psum_pool(name="psum", bufs=PSUM_BANKS))
         ctx.enter_context(tc.manual_schedule())
 
         w_codes = keep.tile([P, CLS], U32, name="w_codes", align_bytes=64)
@@ -59,30 +64,32 @@ def tile_gcnnodeclassifiernetwork_pb_kernel(
         a_codes = keep.tile([P, CHUNKS, NODES], U32, name="a_codes", align_bytes=64)
         a_scales = keep.tile([P, CHUNKS, NODES], U8, name="a_scales", align_bytes=64)
         y = keep.tile([P, TILES, CLS], F32, name="y")
+
         d_col = const.tile([P, TILES], F32, name="d_col")
         slope = const.tile([P, 1], F32, name="slope")
         ident_f32 = const.tile([P, P], F32, name="ident_f32")
         ident_bf = const.tile([P, P], BF16, name="ident_bf")
         ones = const.tile([P, P], BF16, name="ones")
-        w_raw = raw_pool.tile([P, PACK, CLS], BF16, name="w_raw", tag="a_raw")
         d_rows = const.tile([P, P], BF16, name="d_rows")
         b2_rows = const.tile([P, CLS], BF16, name="b2_rows")
         slope_bf = const.tile([P, 1], BF16, name="slope_bf")
+        w_raw = raw_pool.tile([P, PACK, CLS], BF16, name="w_raw", tag="a_raw")
+        w_grp = grp_pool.tile([P, CLS, PACK], BF16, name="w_grp", tag="a_grp", align_bytes=64)
 
         h1_tiles = {}
+        x_tiles = {}
         a_tiles = {}
         h_grps = {}
         u_tiles = {}
+        xb_banks = {}
         m_grps = {}
         a_grps = {}
         acc = {}
-        x_tiles = {}
-        xb_tiles = {}
 
         def load_small():
             nc.vector.memset(d_rows[:], 0.0)
             nc.scalar.dma_start(
-                out=d_rows[0:TILES, :], in_=deg_inv_sqrt.rearrange("(t p) -> t p", p=P)
+                out=d_rows[0:TILES, :], in_=deg_inv_sqrt.rearrange("(n p) -> n p", p=P)
             )
             nc.vector.memset(b2_rows[:], 0.0)
             nc.vector.memset(ones[:], 1.0)
@@ -93,35 +100,35 @@ def tile_gcnnodeclassifiernetwork_pb_kernel(
             for u in range(2):
                 nc.sync.dma_start(
                     out=w_raw[:, 2 * u : 2 * u + 2, :],
-                    in_=W2[u * 256 : (u + 1) * 256, :].rearrange("(q e) c -> q e c", e=2),
+                    in_=W2[u * 2 * P : (u + 1) * 2 * P, :].rearrange("(q e) c -> q e c", e=2),
                 )
 
         def load_h1(c):
-            h1_sb = h1_pool.tile([P, PACK, HID], BF16, name="h1_sb")
+            h1_sb = in_pool.tile([P, PACK, HID], BF16, name="h1_sb")
             nc.sync.dma_start(
                 out=h1_sb[:],
                 in_=h1[c * K_PASS : (c + 1) * K_PASS, :].rearrange("(t p) k -> p t k", p=P),
             )
             h1_tiles[c] = h1_sb
 
-        def load_a(k):
-            r, c = divmod(k, CHUNKS)
-            a_raw = raw_pool.tile([P, PACK, SUB], BF16, name="a_raw")
-            nc.sync.dma_start(
-                out=a_raw[:],
-                in_=A[c * K_PASS : (c + 1) * K_PASS, r * SUB : (r + 1) * SUB].rearrange(
-                    "(t p) w -> p t w", p=P
-                ),
-            )
-            a_tiles[k] = a_raw
-
         def load_x(c):
-            x_sb = h1_pool.tile([P, PACK, CLS], BF16, name="x_sb")
+            x_sb = in_pool.tile([P, PACK, CLS], BF16, name="x_sb")
             nc.sync.dma_start(
                 out=x_sb[:],
                 in_=x[c * K_PASS : (c + 1) * K_PASS, :].rearrange("(t p) k -> p t k", p=P),
             )
             x_tiles[c] = x_sb
+
+        def load_a(k):
+            r, c = divmod(k, CHUNKS)
+            a_raw = raw_pool.tile([P, PACK, ROUND], BF16, name="a_raw")
+            nc.sync.dma_start(
+                out=a_raw[:],
+                in_=A[c * K_PASS : (c + 1) * K_PASS, r * ROUND : (r + 1) * ROUND].rearrange(
+                    "(t p) w -> p t w", p=P
+                ),
+            )
+            a_tiles[k] = a_raw
 
         def warm_sigmoid():
             warm = const.tile([P, 1], F32, name="warm")
@@ -136,10 +143,8 @@ def tile_gcnnodeclassifiernetwork_pb_kernel(
             nc.vector.tensor_copy(out=d_col[:], in_=d_ps[:, 0:TILES])
             nc.vector.tensor_copy(out=slope[:], in_=slope_bf[:])
 
-        w_grp = grp_pool.tile([P, CLS, PACK], BF16, name="w_grp", tag="a_grp", align_bytes=64)
-
         def regroup_w2():
-            w_dst, w_src = interleave(w_grp[:], w_raw[:])
+            w_dst, w_src = side_by_side(w_grp[:], w_raw[:])
             nc.vector.tensor_copy(out=w_dst, in_=w_src)
 
         def quantise_w2():
@@ -200,11 +205,12 @@ def tile_gcnnodeclassifiernetwork_pb_kernel(
 
         def skip_and_bias(c):
             for t in range(PACK):
-                n = c * PACK + t
                 xb_ps = psum.tile([P, CLS], F32, name="xb_ps", tag="bank")
-                nc.tensor.matmul(xb_ps[:], lhsT=ident_bf[:], rhs=x_tiles[c][:, t, :], start=True, stop=False)
+                nc.tensor.matmul(
+                    xb_ps[:], lhsT=ident_bf[:], rhs=x_tiles[c][:, t, :], start=True, stop=False
+                )
                 nc.tensor.matmul(xb_ps[:], lhsT=ones[:], rhs=b2_rows[:], start=False, stop=True)
-                xb_tiles[n] = xb_ps
+                xb_banks[c * PACK + t] = xb_ps
 
         def self_loop(c):
             for t in range(PACK):
@@ -213,14 +219,14 @@ def tile_gcnnodeclassifiernetwork_pb_kernel(
                     out=y[:, n, :],
                     in0=u_tiles[c][:, t, :],
                     scalar=d_col[:, n : n + 1],
-                    in1=xb_tiles[n][:],
+                    in1=xb_banks[n][:],
                     op0=ALU.mult,
                     op1=ALU.add,
                 )
 
         def regroup_m(c):
             m_grp = mid_pool.tile([P, CLS, PACK], BF16, name="m_grp", align_bytes=64)
-            m_dst, m_src = interleave(m_grp[:], u_tiles[c][:])
+            m_dst, m_src = side_by_side(m_grp[:], u_tiles[c][:])
             nc.vector.tensor_copy(out=m_dst, in_=m_src)
             m_grps[c] = m_grp
 
@@ -233,16 +239,16 @@ def tile_gcnnodeclassifiernetwork_pb_kernel(
 
         def regroup_a(k):
             a_raw = a_tiles[k]
-            a_grp = grp_pool.tile([P, SUB, PACK], BF16, name="a_grp", align_bytes=64)
-            s_dst, s_src = interleave(a_grp[:, VEC_COLS:SUB, :], a_raw[:, :, VEC_COLS:SUB])
+            a_grp = grp_pool.tile([P, ROUND, PACK], BF16, name="a_grp", align_bytes=64)
+            s_dst, s_src = side_by_side(a_grp[:, VEC_COLS:ROUND, :], a_raw[:, :, VEC_COLS:ROUND])
             nc.scalar.copy(out=s_dst, in_=s_src)
-            v_dst, v_src = interleave(a_grp[:, 0:VEC_COLS, :], a_raw[:, :, 0:VEC_COLS])
+            v_dst, v_src = side_by_side(a_grp[:, 0:VEC_COLS, :], a_raw[:, :, 0:VEC_COLS])
             nc.vector.tensor_copy(out=v_dst, in_=v_src)
             a_grps[k] = a_grp
 
         def quantise_a(k):
             r, c = divmod(k, CHUNKS)
-            cols = slice(r * SUB, (r + 1) * SUB)
+            cols = slice(r * ROUND, (r + 1) * ROUND)
             nc.vector.quantize_mx(
                 out=a_codes[:, c, cols].bitcast(FP8X4),
                 scales=a_scales[:, c, cols],
@@ -251,13 +257,13 @@ def tile_gcnnodeclassifiernetwork_pb_kernel(
 
         def second_matmul(k):
             r, c = divmod(k, CHUNKS)
-            for j in range(SUB_TILES):
-                jt = r * SUB_TILES + j
+            for j in range(ROUND_TILES):
+                n = r * ROUND_TILES + j
                 if c == 0:
-                    acc[jt] = psum.tile([P, CLS], F32, name="acc", tag="bank")
-                cols = slice(jt * P, (jt + 1) * P)
+                    acc[n] = psum.tile([P, CLS], F32, name="acc", tag="bank")
+                cols = slice(n * P, (n + 1) * P)
                 nc.tensor.matmul_mx(
-                    out=acc[jt][:],
+                    out=acc[n][:],
                     lhsT=a_codes[:, c, cols].bitcast(FP8X4),
                     lhsT_scale=a_scales[:, c, cols],
                     rhs=m_codes[:, c, :].bitcast(FP8X4),
@@ -266,21 +272,19 @@ def tile_gcnnodeclassifiernetwork_pb_kernel(
                     stop=(c == CHUNKS - 1),
                 )
 
-        def finish(jt):
+        def finish(n):
             res = res_pool.tile([P, CLS], F32, name="res")
             nc.vector.scalar_tensor_tensor(
                 out=res[:],
-                in0=acc[jt][:],
-                scalar=d_col[:, jt : jt + 1],
-                in1=y[:, jt, :],
+                in0=acc[n][:],
+                scalar=d_col[:, n : n + 1],
+                in1=y[:, n, :],
                 op0=ALU.mult,
                 op1=ALU.add,
             )
             nc.scalar.activation(out=res[:], in_=res[:], func=ACT.Sigmoid, scale=slope[:, 0:1])
-            nc.sync.dma_start(out=out[jt * P : (jt + 1) * P, :], in_=res[:])
+            nc.sync.dma_start(out=out[n * P : (n + 1) * P, :], in_=res[:])
 
-        LEAD = 6
-        LAG = 5
         load_small()
         load_h1(0)
         load_w2()
@@ -293,8 +297,9 @@ def tile_gcnnodeclassifiernetwork_pb_kernel(
         transpose_h1(0)
         spread_small()
         regroup_w2()
-        quantise_w2()
         quantise_h1(0)
+        quantise_w2()
+
         for c in range(CHUNKS):
             if c + 2 < CHUNKS:
                 load_h1(c + 2)
@@ -319,6 +324,7 @@ def tile_gcnnodeclassifiernetwork_pb_kernel(
         quantise_m(CHUNKS - 1)
         for k in range(CHUNKS, LEAD):
             regroup_a(k)
+
         for k in range(SUBS + LAG):
             if k < SUBS:
                 quantise_a(k)

@@ -141,7 +141,6 @@ def tile_gcnnodeclassifiernetwork_pb_kernel(
             d_ps = psum.tile([P, P], BF16, name="d_ps", tag="bank")
             nc.tensor.transpose(d_ps[:], d_rows[:], ident_bf[:])
             nc.vector.tensor_copy(out=d_col[:], in_=d_ps[:, 0:TILES])
-            nc.vector.tensor_copy(out=slope[:], in_=slope_bf[:])
 
         def regroup_w2():
             w_dst, w_src = side_by_side(w_grp[:], w_raw[:])
@@ -322,6 +321,7 @@ def tile_gcnnodeclassifiernetwork_pb_kernel(
             load_a(k)
         regroup_m(CHUNKS - 1)
         quantise_m(CHUNKS - 1)
+        nc.vector.tensor_copy(out=slope[:], in_=slope_bf[:])
         for k in range(CHUNKS, LEAD):
             regroup_a(k)
 

@@ -236,14 +236,46 @@ def tile_gcnnodeclassifiernetwork_pb_kernel(
                 in_=m_grps[c][:].rearrange("p w t -> p (w t)"),
             )
 
-        def regroup_a(k):
-            a_raw = a_tiles[k]
-            a_grp = grp_pool.tile([P, ROUND, PACK], BF16, name="a_grp", align_bytes=64)
-            s_dst, s_src = side_by_side(a_grp[:, VEC_COLS:ROUND, :], a_raw[:, :, VEC_COLS:ROUND])
-            nc.scalar.copy(out=s_dst, in_=s_src)
-            v_dst, v_src = side_by_side(a_grp[:, 0:VEC_COLS, :], a_raw[:, :, 0:VEC_COLS])
-            nc.vector.tensor_copy(out=v_dst, in_=v_src)
-            a_grps[k] = a_grp
+        def grp(k):
+            if k not in a_grps:
+                a_grps[k] = grp_pool.tile([P, ROUND, PACK], BF16, name="a_grp", align_bytes=64)
+            return a_grps[k]
+
+        def shares(k):
+            v = [0,0,0,0,112,112,112,112,112,112,112,112,112,112,112,112][k]
+            g = [384,384,384,384,0,0,0,0,0,0,0,0,0,0,0,0][k]
+            return v, g
+
+        def regroup_s(k):
+            v, g = shares(k)
+            cols = slice(v, ROUND - g)
+            if v < ROUND - g:
+                s_dst, s_src = side_by_side(grp(k)[:, cols, :], a_tiles[k][:, :, cols])
+                nc.scalar.copy(out=s_dst, in_=s_src)
+
+        def regroup_v(k):
+            v, g = shares(k)
+            if v > 0:
+                v_dst, v_src = side_by_side(grp(k)[:, 0:v, :], a_tiles[k][:, :, 0:v])
+                nc.vector.tensor_copy(out=v_dst, in_=v_src)
+
+        def regroup_g(k, go_t):
+            v, g = shares(k)
+            cols = slice(ROUND - g, ROUND)
+            if g > 0:
+                nc.gpsimd.tensor_scalar(
+                    out=grp(k)[:, cols, :],
+                    in0=a_tiles[k][:, :, cols].rearrange("p t w -> p w t"),
+                    scalar1=go_t[:, 0:1],
+                    scalar2=0.0,
+                    op0=ALU.mult,
+                    op1=ALU.add,
+                )
+
+        def go():
+            t = mid_pool.tile([P, 1], F32, name="go_t", bufs=4)
+            nc.vector.memset(t[:], 1.0)
+            return t
 
         def quantise_a(k):
             r, c = divmod(k, CHUNKS)
@@ -294,8 +326,8 @@ def tile_gcnnodeclassifiernetwork_pb_kernel(
         warm_sigmoid()
         make_identity(nc, ident_f32[:])
         transpose_h1(0)
-        spread_small()
         regroup_w2()
+        spread_small()
         quantise_h1(0)
         quantise_w2()
 
@@ -315,21 +347,37 @@ def tile_gcnnodeclassifiernetwork_pb_kernel(
                 quantise_h1(c + 1)
             if c > 0:
                 quantise_m(c - 1)
+            t = go()
+            for k in [[0],[1],[2],[3]][c]:
+                regroup_g(k, t)
             self_loop(c)
-            regroup_a(c)
+            for k in [[],[],[],[]][c]:
+                regroup_v(k)
+            for k in [[0],[1],[2],[3]][c]:
+                regroup_s(k)
         for k in range(CHUNKS + 1, SUBS):
             load_a(k)
         regroup_m(CHUNKS - 1)
         quantise_m(CHUNKS - 1)
         nc.vector.tensor_copy(out=slope[:], in_=slope_bf[:])
-        for k in range(CHUNKS, LEAD):
-            regroup_a(k)
+        for k in [4,5]:
+            regroup_s(k)
+        for k in [4,5]:
+            regroup_v(k)
 
-        for k in range(SUBS + LAG):
-            if k < SUBS:
-                quantise_a(k)
-                second_matmul(k)
-            if k + LEAD < SUBS:
-                regroup_a(k + LEAD)
-            if k >= LAG:
-                finish(k - LAG)
+        for r in range(ROUNDS + 1):
+            for i in range(CHUNKS):
+                k = r * CHUNKS + i
+                if k < SUBS:
+                    quantise_a(k)
+                    second_matmul(k)
+                    if k + 6 < SUBS:
+                        regroup_v(k + 6)
+                    if k + 6 < SUBS:
+                        regroup_s(k + 6)
+            if r > 0:
+                t = go()
+                for k in {}.get(r, []):
+                    regroup_g(k, t)
+                for i in range(CHUNKS):
+                    finish((r - 1) * CHUNKS + i)

@@ -103,13 +103,15 @@ def tile_gcnnodeclassifiernetwork_pb_kernel(
                     in_=W2[u * 2 * P : (u + 1) * 2 * P, :].rearrange("(q e) c -> q e c", e=2),
                 )
 
-        def load_h1(c):
-            h1_sb = in_pool.tile([P, PACK, HID], BF16, name="h1_sb")
+        def load_h1(c, pairs=(0, 1)):
+            if c not in h1_tiles:
+                h1_tiles[c] = in_pool.tile([P, PACK, HID], BF16, name="h1_sb")
+            t0, t1 = 2 * pairs[0], 2 * pairs[-1] + 2
+            r0 = c * K_PASS
             nc.sync.dma_start(
-                out=h1_sb[:],
-                in_=h1[c * K_PASS : (c + 1) * K_PASS, :].rearrange("(t p) k -> p t k", p=P),
+                out=h1_tiles[c][:, t0:t1, :],
+                in_=h1[r0 + t0 * P : r0 + t1 * P, :].rearrange("(t p) k -> p t k", p=P),
             )
-            h1_tiles[c] = h1_sb
 
         def load_x(c):
             x_sb = in_pool.tile([P, PACK, CLS], BF16, name="x_sb")
@@ -136,15 +138,19 @@ def tile_gcnnodeclassifiernetwork_pb_kernel(
             warm_out = const.tile([P, 1], F32, name="warm_out")
             nc.scalar.activation(out=warm_out[:], in_=warm[:], func=ACT.Sigmoid)
 
-        def spread_small():
+        def bf_identity():
             nc.vector.tensor_copy(out=ident_bf[:], in_=ident_f32[:])
+
+        def spread_small():
             d_ps = psum.tile([P, P], BF16, name="d_ps", tag="bank")
             nc.tensor.transpose(d_ps[:], d_rows[:], ident_bf[:])
             nc.vector.tensor_copy(out=d_col[:], in_=d_ps[:, 0:TILES])
 
         def regroup_w2():
-            w_dst, w_src = side_by_side(w_grp[:], w_raw[:])
+            w_dst, w_src = side_by_side(w_grp[:, 0:352, :], w_raw[:, :, 0:352])
             nc.vector.tensor_copy(out=w_dst, in_=w_src)
+            w_dst, w_src = side_by_side(w_grp[:, 352:CLS, :], w_raw[:, :, 352:CLS])
+            nc.scalar.copy(out=w_dst, in_=w_src)
 
         def quantise_w2():
             nc.vector.quantize_mx(
@@ -153,11 +159,12 @@ def tile_gcnnodeclassifiernetwork_pb_kernel(
                 in_=w_grp[:].rearrange("p c t -> p (c t)"),
             )
 
-        def transpose_h1(c):
+        def transpose_h1(c, pairs=(0, 1)):
             h1_words = h1_tiles[c][:].bitcast(F32)
-            h_grp = mid_pool.tile([P, K_PASS, PACK], BF16, name="h_grp", align_bytes=64)
-            h_grp_words = h_grp[:].bitcast(F32)
-            for pair in range(2):
+            if c not in h_grps:
+                h_grps[c] = mid_pool.tile([P, K_PASS, PACK], BF16, name="h_grp", align_bytes=64)
+            h_grp_words = h_grps[c][:].bitcast(F32)
+            for pair in pairs:
                 xt = psum.tile([P, 2, 2, P], F32, name="xt", tag="bank")
                 for s in range(2):
                     for u in range(2):
@@ -172,7 +179,6 @@ def tile_gcnnodeclassifiernetwork_pb_kernel(
                     ),
                     in_=xt[:].rearrange("p s u r -> p s r u"),
                 )
-            h_grps[c] = h_grp
 
         def quantise_h1(c):
             cols = slice(c * K_PASS, (c + 1) * K_PASS)
@@ -202,8 +208,8 @@ def tile_gcnnodeclassifiernetwork_pb_kernel(
                 )
             u_tiles[c] = u_sb
 
-        def skip_and_bias(c):
-            for t in range(PACK):
+        def skip_and_bias(c, tiles=(0, 1, 2, 3)):
+            for t in tiles:
                 xb_ps = psum.tile([P, CLS], F32, name="xb_ps", tag="bank")
                 nc.tensor.matmul(
                     xb_ps[:], lhsT=ident_bf[:], rhs=x_tiles[c][:, t, :], start=True, stop=False
@@ -242,8 +248,8 @@ def tile_gcnnodeclassifiernetwork_pb_kernel(
             return a_grps[k]
 
         def shares(k):
-            v = [0,0,0,0,112,112,112,112,112,112,112,112,112,112,112,112][k]
-            g = [384,384,384,384,0,0,0,0,0,0,0,0,0,0,0,0][k]
+            v = [0,0,0,0,128,128,128,128,128,128,0,128,128,128,0,128][k]
+            g = [384,384,384,384,0,0,0,0,0,0,320,0,0,0,320,0][k]
             return v, g
 
         def regroup_s(k):
@@ -317,19 +323,22 @@ def tile_gcnnodeclassifiernetwork_pb_kernel(
             nc.sync.dma_start(out=out[n * P : (n + 1) * P, :], in_=res[:])
 
         load_small()
-        load_h1(0)
+        load_h1(0, (0,))
         load_w2()
-        load_h1(1)
+        load_h1(0, (1,))
         load_x(0)
+        load_h1(1)
         load_a(0)
         load_x(1)
         warm_sigmoid()
         make_identity(nc, ident_f32[:])
-        transpose_h1(0)
+        bf_identity()
+        transpose_h1(0, (0,))
         regroup_w2()
+        transpose_h1(0, (1,))
         spread_small()
-        quantise_h1(0)
         quantise_w2()
+        quantise_h1(0)
 
         for c in range(CHUNKS):
             if c + 2 < CHUNKS:
@@ -337,20 +346,27 @@ def tile_gcnnodeclassifiernetwork_pb_kernel(
             load_a(c + 1)
             if c + 2 < CHUNKS:
                 load_x(c + 2)
-            if c + 1 < CHUNKS:
-                transpose_h1(c + 1)
-            first_matmul(c)
-            skip_and_bias(c)
-            if c > 0:
+            if c == 0:
+                skip_and_bias(0, (0,))
+                first_matmul(0)
+                skip_and_bias(0, (1,))
+                transpose_h1(1)
+                skip_and_bias(0, (2, 3))
+            else:
+                if c + 1 < CHUNKS:
+                    transpose_h1(c + 1)
+                first_matmul(c)
+                skip_and_bias(c)
                 regroup_m(c - 1)
-            if c + 1 < CHUNKS:
-                quantise_h1(c + 1)
-            if c > 0:
+                if c + 1 < CHUNKS:
+                    quantise_h1(c + 1)
                 quantise_m(c - 1)
             t = go()
             for k in [[0],[1],[2],[3]][c]:
                 regroup_g(k, t)
             self_loop(c)
+            if c == 0:
+                quantise_h1(1)
             for k in [[],[],[],[]][c]:
                 regroup_v(k)
             for k in [[0],[1],[2],[3]][c]:
@@ -377,7 +393,7 @@ def tile_gcnnodeclassifiernetwork_pb_kernel(
                         regroup_s(k + 6)
             if r > 0:
                 t = go()
-                for k in {}.get(r, []):
+                for k in {1:[10],2:[14]}.get(r, []):
                     regroup_g(k, t)
                 for i in range(CHUNKS):
                     finish((r - 1) * CHUNKS + i)

@@ -248,8 +248,8 @@ def tile_gcnnodeclassifiernetwork_pb_kernel(
             return a_grps[k]
 
         def shares(k):
-            v = [0,0,0,0,128,128,128,128,128,128,0,128,128,128,0,128][k]
-            g = [384,384,384,384,0,0,0,0,0,0,320,0,0,0,320,0][k]
+            v = [0,0,0,0,0,0,512,0,256,0,0,512,0,0,0,0][k]
+            g = [384,384,384,384,0,0,0,0,0,0,384,0,0,0,384,160][k]
             return v, g
 
         def regroup_s(k):
@@ -265,23 +265,22 @@ def tile_gcnnodeclassifiernetwork_pb_kernel(
                 v_dst, v_src = side_by_side(grp(k)[:, 0:v, :], a_tiles[k][:, :, 0:v])
                 nc.vector.tensor_copy(out=v_dst, in_=v_src)
 
-        def regroup_g(k, go_t):
+        def regroup_g(k):
             v, g = shares(k)
             cols = slice(ROUND - g, ROUND)
             if g > 0:
                 nc.gpsimd.tensor_scalar(
                     out=grp(k)[:, cols, :],
                     in0=a_tiles[k][:, :, cols].rearrange("p t w -> p w t"),
-                    scalar1=go_t[:, 0:1],
+                    scalar1=1.0,
                     scalar2=0.0,
                     op0=ALU.mult,
                     op1=ALU.add,
                 )
 
-        def go():
-            t = mid_pool.tile([P, 1], F32, name="go_t", bufs=4)
-            nc.vector.memset(t[:], 1.0)
-            return t
+        def wait_for(ap):
+            t = mid_pool.tile([1, 1], U32, name="seen", bufs=2)
+            nc.gpsimd.tensor_copy(out=t[:], in_=ap)
 
         def quantise_a(k):
             r, c = divmod(k, CHUNKS)
@@ -332,13 +331,14 @@ def tile_gcnnodeclassifiernetwork_pb_kernel(
         load_x(1)
         warm_sigmoid()
         make_identity(nc, ident_f32[:])
+        nc.gpsimd.tensor_copy(out=slope[:], in_=slope_bf[:])
         bf_identity()
         transpose_h1(0, (0,))
         regroup_w2()
         transpose_h1(0, (1,))
-        spread_small()
         quantise_w2()
         quantise_h1(0)
+        spread_small()
 
         for c in range(CHUNKS):
             if c + 2 < CHUNKS:
@@ -361,9 +361,8 @@ def tile_gcnnodeclassifiernetwork_pb_kernel(
                 if c + 1 < CHUNKS:
                     quantise_h1(c + 1)
                 quantise_m(c - 1)
-            t = go()
-            for k in [[0],[1],[2],[3]][c]:
-                regroup_g(k, t)
+            wait_for(h_codes[0:1, 0:1] if c == 0 else m_codes[0:1, c - 1, 0:1])
+            regroup_g(c)
             self_loop(c)
             if c == 0:
                 quantise_h1(1)
@@ -375,25 +374,30 @@ def tile_gcnnodeclassifiernetwork_pb_kernel(
             load_a(k)
         regroup_m(CHUNKS - 1)
         quantise_m(CHUNKS - 1)
-        nc.vector.tensor_copy(out=slope[:], in_=slope_bf[:])
         for k in [4,5]:
             regroup_s(k)
-        for k in [4,5]:
-            regroup_v(k)
 
-        for r in range(ROUNDS + 1):
-            for i in range(CHUNKS):
-                k = r * CHUNKS + i
-                if k < SUBS:
-                    quantise_a(k)
-                    second_matmul(k)
-                    if k + 6 < SUBS:
-                        regroup_v(k + 6)
-                    if k + 6 < SUBS:
-                        regroup_s(k + 6)
-            if r > 0:
-                t = go()
-                for k in {1:[10],2:[14]}.get(r, []):
-                    regroup_g(k, t)
-                for i in range(CHUNKS):
-                    finish((r - 1) * CHUNKS + i)
+        VEC_AT = {2: 6, 4: 8, 6: 11}
+        for k in range(SUBS):
+            r, i = divmod(k, CHUNKS)
+            if k == SUBS - 1:
+                wait_for(a_codes[0:1, 2, 3 * ROUND : 3 * ROUND + 1])
+                regroup_g(15)
+                finish(8)
+                finish(9)
+            quantise_a(k)
+            second_matmul(k)
+            if k in VEC_AT:
+                regroup_v(VEC_AT[k])
+            if k + 6 < SUBS:
+                regroup_s(k + 6)
+            if k == SUBS - 1:
+                finish(10)
+                finish(11)
+            elif r > 0 and i == CHUNKS - 1:
+                wait_for(a_codes[0:1, i, r * ROUND : r * ROUND + 1])
+                regroup_g({1: 10, 2: 14}[r])
+                for n in range(CHUNKS):
+                    finish((r - 1) * CHUNKS + n)
+        for n in range(CHUNKS):
+            finish(SUBS - CHUNKS + n)

@@ -249,7 +249,7 @@ def tile_gcnnodeclassifiernetwork_pb_kernel(
 
         def shares(k):
             v = [0,0,0,0,0,0,512,0,256,0,0,512,0,0,0,0][k]
-            g = [384,384,384,384,0,0,0,0,0,0,384,0,0,0,384,160][k]
+            g = [320,320,320,320,0,0,0,0,0,0,320,0,0,0,320,128][k]
             return v, g
 
         def regroup_s(k):

@@ -110,7 +110,7 @@ def tile_gcnnodeclassifiernetwork_pb_kernel(
             r0 = c * K_PASS
             nc.sync.dma_start(
                 out=h1_tiles[c][:, t0:t1, :],
-                in_=h1[r0 + t0 * P : r0 + t1 * P, :].rearrange("(t p) k -> p t k", p=P),
+                in_=h1[r0 : r0 + K_PASS, :].rearrange("(p t) k -> p t k", t=PACK)[:, t0:t1, :],
             )
 
         def load_x(c):
@@ -174,10 +174,8 @@ def tile_gcnnodeclassifiernetwork_pb_kernel(
                             ident_f32[:],
                         )
                 nc.scalar.copy(
-                    out=h_grp_words[:, pair * 2 * P : (pair + 1) * 2 * P, :].rearrange(
-                        "p (s r) u -> p s r u", s=2
-                    ),
-                    in_=xt[:].rearrange("p s u r -> p s r u"),
+                    out=h_grp_words.rearrange("p (r t) u -> p r t u", t=PACK)[:, :, 2 * pair : 2 * pair + 2, :],
+                    in_=xt[:].rearrange("p s u r -> p r s u"),
                 )
 
         def quantise_h1(c):
@@ -248,7 +246,7 @@ def tile_gcnnodeclassifiernetwork_pb_kernel(
             return a_grps[k]
 
         def shares(k):
-            v = [0,0,0,0,0,0,512,0,256,0,0,512,0,0,0,0][k]
+            v = [0,0,0,0,0,0,512,0,320,0,0,512,0,0,0,0][k]
             g = [320,320,320,320,0,0,0,0,0,0,320,0,0,0,320,128][k]
             return v, g
 

from contextlib import ExitStack

import concourse.mybir as mybir
from concourse.masks import make_identity

F32 = mybir.dt.float32
BF16 = mybir.dt.bfloat16
U32 = mybir.dt.uint32
U8 = mybir.dt.uint8
FP8X4 = mybir.dt.float8_e4m3fn_x4
ACT = mybir.ActivationFunctionType
ALU = mybir.AluOpType

P = 128
PACK = 4
K_PASS = P * PACK
NODES = 2048
HID = 512
CLS = 512
TILES = NODES // P
CHUNKS = NODES // K_PASS
ROUND = 512
ROUND_TILES = ROUND // P
ROUNDS = NODES // ROUND
SUBS = ROUNDS * CHUNKS
PSUM_BANKS = 8

VEC_COLS = 176
LEAD = 6
LAG = CHUNKS + 1
assert TILES == SUBS

FLOPS = 2 * NODES * HID * CLS + 2 * NODES * NODES * CLS


def side_by_side(dst, src):
    return (
        dst.rearrange("p (c i) t -> p c t i", i=4),
        src.rearrange("p t (c i) -> p c t i", i=4),
    )


def tile_gcnnodeclassifiernetwork_pb_kernel(
    tc, A, deg_inv_sqrt, h1, W2, b2, x, sigmoid_param, out
):
    nc = tc.nc
    with ExitStack() as ctx:
        const = ctx.enter_context(tc.tile_pool(name="const", bufs=1))
        keep = ctx.enter_context(tc.tile_pool(name="keep", bufs=1))
        in_pool = ctx.enter_context(tc.tile_pool(name="in_pool", bufs=2))
        raw_pool = ctx.enter_context(tc.tile_pool(name="raw_pool", bufs=LEAD + 2))
        grp_pool = ctx.enter_context(tc.tile_pool(name="grp_pool", bufs=LEAD + 2))
        mid_pool = ctx.enter_context(tc.tile_pool(name="mid_pool", bufs=2))
        res_pool = ctx.enter_context(tc.tile_pool(name="res_pool", bufs=8))
        psum = ctx.enter_context(tc.psum_pool(name="psum", bufs=PSUM_BANKS))
        ctx.enter_context(tc.manual_schedule())

        w_codes = keep.tile([P, CLS], U32, name="w_codes", align_bytes=64)
        w_scales = keep.tile([P, CLS], U8, name="w_scales", align_bytes=64)
        h_codes = keep.tile([P, NODES], U32, name="h_codes", align_bytes=64)
        h_scales = keep.tile([P, NODES], U8, name="h_scales", align_bytes=64)
        m_codes = keep.tile([P, CHUNKS, CLS], U32, name="m_codes", align_bytes=64)
        m_scales = keep.tile([P, CHUNKS, CLS], U8, name="m_scales", align_bytes=64)
        a_codes = keep.tile([P, CHUNKS, NODES], U32, name="a_codes", align_bytes=64)
        a_scales = keep.tile([P, CHUNKS, NODES], U8, name="a_scales", align_bytes=64)
        y = keep.tile([P, TILES, CLS], F32, name="y")

        d_col = const.tile([P, TILES], F32, name="d_col")
        slope = const.tile([P, 1], F32, name="slope")
        ident_f32 = const.tile([P, P], F32, name="ident_f32")
        ident_bf = const.tile([P, P], BF16, name="ident_bf")
        ones = const.tile([P, P], BF16, name="ones")
        d_rows = const.tile([P, P], BF16, name="d_rows")
        b2_rows = const.tile([P, CLS], BF16, name="b2_rows")
        slope_bf = const.tile([P, 1], BF16, name="slope_bf")
        w_raw = raw_pool.tile([P, PACK, CLS], BF16, name="w_raw", tag="a_raw")
        w_grp = grp_pool.tile([P, CLS, PACK], BF16, name="w_grp", tag="a_grp", align_bytes=64)

        h1_tiles = {}
        x_tiles = {}
        a_tiles = {}
        h_grps = {}
        u_tiles = {}
        xb_banks = {}
        m_grps = {}
        a_grps = {}
        acc = {}

        def load_small():
            nc.vector.memset(d_rows[:], 0.0)
            nc.scalar.dma_start(
                out=d_rows[0:TILES, :], in_=deg_inv_sqrt.rearrange("(n p) -> n p", p=P)
            )
            nc.vector.memset(b2_rows[:], 0.0)
            nc.vector.memset(ones[:], 1.0)
            nc.scalar.dma_start(out=b2_rows[0:1, :], in_=b2.unsqueeze(0))
            nc.scalar.dma_start(out=slope_bf[:], in_=sigmoid_param.partition_broadcast(P))

        def load_w2():
            for u in range(2):
                nc.sync.dma_start(
                    out=w_raw[:, 2 * u : 2 * u + 2, :],
                    in_=W2[u * 2 * P : (u + 1) * 2 * P, :].rearrange("(q e) c -> q e c", e=2),
                )

        def load_h1(c, pairs=(0, 1)):
            if c not in h1_tiles:
                h1_tiles[c] = in_pool.tile([P, PACK, HID], BF16, name="h1_sb")
            t0, t1 = 2 * pairs[0], 2 * pairs[-1] + 2
            r0 = c * K_PASS
            nc.sync.dma_start(
                out=h1_tiles[c][:, t0:t1, :],
                in_=h1[r0 : r0 + K_PASS, :].rearrange("(p t) k -> p t k", t=PACK)[:, t0:t1, :],
            )

        def load_x(c):
            x_sb = in_pool.tile([P, PACK, CLS], BF16, name="x_sb")
            nc.sync.dma_start(
                out=x_sb[:],
                in_=x[c * K_PASS : (c + 1) * K_PASS, :].rearrange("(t p) k -> p t k", p=P),
            )
            x_tiles[c] = x_sb

        def load_a(k):
            r, c = divmod(k, CHUNKS)
            a_raw = raw_pool.tile([P, PACK, ROUND], BF16, name="a_raw")
            nc.sync.dma_start(
                out=a_raw[:],
                in_=A[c * K_PASS : (c + 1) * K_PASS, r * ROUND : (r + 1) * ROUND].rearrange(
                    "(t p) w -> p t w", p=P
                ),
            )
            a_tiles[k] = a_raw

        def warm_sigmoid():
            warm = const.tile([P, 1], F32, name="warm")
            nc.vector.memset(warm[:], 0.0)
            warm_out = const.tile([P, 1], F32, name="warm_out")
            nc.scalar.activation(out=warm_out[:], in_=warm[:], func=ACT.Sigmoid)

        def bf_identity():
            nc.vector.tensor_copy(out=ident_bf[:], in_=ident_f32[:])

        def spread_small():
            d_ps = psum.tile([P, P], BF16, name="d_ps", tag="bank")
            nc.tensor.transpose(d_ps[:], d_rows[:], ident_bf[:])
            nc.vector.tensor_copy(out=d_col[:], in_=d_ps[:, 0:TILES])

        def regroup_w2():
            w_dst, w_src = side_by_side(w_grp[:, 0:352, :], w_raw[:, :, 0:352])
            nc.vector.tensor_copy(out=w_dst, in_=w_src)
            w_dst, w_src = side_by_side(w_grp[:, 352:CLS, :], w_raw[:, :, 352:CLS])
            nc.scalar.copy(out=w_dst, in_=w_src)

        def quantise_w2():
            nc.vector.quantize_mx(
                out=w_codes[:].bitcast(FP8X4),
                scales=w_scales[:],
                in_=w_grp[:].rearrange("p c t -> p (c t)"),
            )

        def transpose_h1(c, pairs=(0, 1)):
            h1_words = h1_tiles[c][:].bitcast(F32)
            if c not in h_grps:
                h_grps[c] = mid_pool.tile([P, K_PASS, PACK], BF16, name="h_grp", align_bytes=64)
            h_grp_words = h_grps[c][:].bitcast(F32)
            for pair in pairs:
                xt = psum.tile([P, 2, 2, P], F32, name="xt", tag="bank")
                for s in range(2):
                    for u in range(2):
                        nc.tensor.transpose(
                            xt[:, s, u, :],
                            h1_words[:, 2 * pair + s, u * P : (u + 1) * P],
                            ident_f32[:],
                        )
                nc.scalar.copy(
                    out=h_grp_words.rearrange("p (r t) u -> p r t u", t=PACK)[:, :, 2 * pair : 2 * pair + 2, :],
                    in_=xt[:].rearrange("p s u r -> p r s u"),
                )

        def quantise_h1(c):
            cols = slice(c * K_PASS, (c + 1) * K_PASS)
            nc.vector.quantize_mx(
                out=h_codes[:, cols].bitcast(FP8X4),
                scales=h_scales[:, cols],
                in_=h_grps[c][:].rearrange("p r t -> p (r t)"),
            )

        def first_matmul(c):
            u_sb = mid_pool.tile([P, PACK, CLS], F32, name="u_sb")
            for t in range(PACK):
                n = c * PACK + t
                cols = slice(n * P, (n + 1) * P)
                g_ps = psum.tile([P, CLS], F32, name="g_ps", tag="bank")
                nc.tensor.matmul_mx(
                    out=g_ps[:],
                    lhsT=h_codes[:, cols].bitcast(FP8X4),
                    lhsT_scale=h_scales[:, cols],
                    rhs=w_codes[:].bitcast(FP8X4),
                    rhs_scale=w_scales[:],
                    start=True,
                    stop=True,
                )
                nc.scalar.activation(
                    out=u_sb[:, t, :], in_=g_ps[:], func=ACT.Copy, scale=d_col[:, n : n + 1]
                )
            u_tiles[c] = u_sb

        def skip_and_bias(c, tiles=(0, 1, 2, 3)):
            for t in tiles:
                xb_ps = psum.tile([P, CLS], F32, name="xb_ps", tag="bank")
                nc.tensor.matmul(
                    xb_ps[:], lhsT=ident_bf[:], rhs=x_tiles[c][:, t, :], start=True, stop=False
                )
                nc.tensor.matmul(xb_ps[:], lhsT=ones[:], rhs=b2_rows[:], start=False, stop=True)
                xb_banks[c * PACK + t] = xb_ps

        def self_loop(c):
            for t in range(PACK):
                n = c * PACK + t
                nc.vector.scalar_tensor_tensor(
                    out=y[:, n, :],
                    in0=u_tiles[c][:, t, :],
                    scalar=d_col[:, n : n + 1],
                    in1=xb_banks[n][:],
                    op0=ALU.mult,
                    op1=ALU.add,
                )

        def regroup_m(c):
            m_grp = mid_pool.tile([P, CLS, PACK], BF16, name="m_grp", align_bytes=64)
            m_dst, m_src = side_by_side(m_grp[:], u_tiles[c][:])
            nc.vector.tensor_copy(out=m_dst, in_=m_src)
            m_grps[c] = m_grp

        def quantise_m(c):
            nc.vector.quantize_mx(
                out=m_codes[:, c, :].bitcast(FP8X4),
                scales=m_scales[:, c, :],
                in_=m_grps[c][:].rearrange("p w t -> p (w t)"),
            )

        def grp(k):
            if k not in a_grps:
                a_grps[k] = grp_pool.tile([P, ROUND, PACK], BF16, name="a_grp", align_bytes=64)
            return a_grps[k]

        def shares(k):
            v = [0,0,0,0,0,0,512,0,320,0,0,512,0,0,0,0][k]
            g = [320,320,320,320,0,0,0,0,0,0,320,0,0,0,320,128][k]
            return v, g

        def regroup_s(k):
            v, g = shares(k)
            cols = slice(v, ROUND - g)
            if v < ROUND - g:
                s_dst, s_src = side_by_side(grp(k)[:, cols, :], a_tiles[k][:, :, cols])
                nc.scalar.copy(out=s_dst, in_=s_src)

        def regroup_v(k):
            v, g = shares(k)
            if v > 0:
                v_dst, v_src = side_by_side(grp(k)[:, 0:v, :], a_tiles[k][:, :, 0:v])
                nc.vector.tensor_copy(out=v_dst, in_=v_src)

        def regroup_g(k):
            v, g = shares(k)
            cols = slice(ROUND - g, ROUND)
            if g > 0:
                nc.gpsimd.tensor_scalar(
                    out=grp(k)[:, cols, :],
                    in0=a_tiles[k][:, :, cols].rearrange("p t w -> p w t"),
                    scalar1=1.0,
                    scalar2=0.0,
                    op0=ALU.mult,
                    op1=ALU.add,
                )

        def wait_for(ap):
            t = mid_pool.tile([1, 1], U32, name="seen", bufs=2)
            nc.gpsimd.tensor_copy(out=t[:], in_=ap)

        def quantise_a(k):
            r, c = divmod(k, CHUNKS)
            cols = slice(r * ROUND, (r + 1) * ROUND)
            nc.vector.quantize_mx(
                out=a_codes[:, c, cols].bitcast(FP8X4),
                scales=a_scales[:, c, cols],
                in_=a_grps[k][:].rearrange("p w t -> p (w t)"),
            )

        def second_matmul(k):
            r, c = divmod(k, CHUNKS)
            for j in range(ROUND_TILES):
                n = r * ROUND_TILES + j
                if c == 0:
                    acc[n] = psum.tile([P, CLS], F32, name="acc", tag="bank")
                cols = slice(n * P, (n + 1) * P)
                nc.tensor.matmul_mx(
                    out=acc[n][:],
                    lhsT=a_codes[:, c, cols].bitcast(FP8X4),
                    lhsT_scale=a_scales[:, c, cols],
                    rhs=m_codes[:, c, :].bitcast(FP8X4),
                    rhs_scale=m_scales[:, c, :],
                    start=(c == 0),
                    stop=(c == CHUNKS - 1),
                )

        def finish(n):
            res = res_pool.tile([P, CLS], F32, name="res")
            nc.vector.scalar_tensor_tensor(
                out=res[:],
                in0=acc[n][:],
                scalar=d_col[:, n : n + 1],
                in1=y[:, n, :],
                op0=ALU.mult,
                op1=ALU.add,
            )
            nc.scalar.activation(out=res[:], in_=res[:], func=ACT.Sigmoid, scale=slope[:, 0:1])
            nc.sync.dma_start(out=out[n * P : (n + 1) * P, :], in_=res[:])

        load_small()
        load_h1(0, (0,))
        load_w2()
        load_h1(0, (1,))
        load_x(0)
        load_h1(1)
        load_a(0)
        load_x(1)
        warm_sigmoid()
        make_identity(nc, ident_f32[:])
        nc.gpsimd.tensor_copy(out=slope[:], in_=slope_bf[:])
        bf_identity()
        transpose_h1(0, (0,))
        regroup_w2()
        transpose_h1(0, (1,))
        quantise_w2()
        quantise_h1(0)
        spread_small()

        for c in range(CHUNKS):
            if c + 2 < CHUNKS:
                load_h1(c + 2)
            load_a(c + 1)
            if c + 2 < CHUNKS:
                load_x(c + 2)
            if c == 0:
                skip_and_bias(0, (0,))
                first_matmul(0)
                skip_and_bias(0, (1,))
                transpose_h1(1)
                skip_and_bias(0, (2, 3))
            else:
                if c + 1 < CHUNKS:
                    transpose_h1(c + 1)
                first_matmul(c)
                skip_and_bias(c)
                regroup_m(c - 1)
                if c + 1 < CHUNKS:
                    quantise_h1(c + 1)
                quantise_m(c - 1)
            wait_for(h_codes[0:1, 0:1] if c == 0 else m_codes[0:1, c - 1, 0:1])
            regroup_g(c)
            self_loop(c)
            if c == 0:
                quantise_h1(1)
            for k in [[],[],[],[]][c]:
                regroup_v(k)
            for k in [[0],[1],[2],[3]][c]:
                regroup_s(k)
        for k in range(CHUNKS + 1, SUBS):
            load_a(k)
        regroup_m(CHUNKS - 1)
        quantise_m(CHUNKS - 1)
        for k in [4,5]:
            regroup_s(k)

        VEC_AT = {2: 6, 4: 8, 6: 11}
        for k in range(SUBS):
            r, i = divmod(k, CHUNKS)
            if k == SUBS - 1:
                wait_for(a_codes[0:1, 2, 3 * ROUND : 3 * ROUND + 1])
                regroup_g(15)
                finish(8)
                finish(9)
            quantise_a(k)
            second_matmul(k)
            if k in VEC_AT:
                regroup_v(VEC_AT[k])
            if k + 6 < SUBS:
                regroup_s(k + 6)
            if k == SUBS - 1:
                finish(10)
                finish(11)
            elif r > 0 and i == CHUNKS - 1:
                wait_for(a_codes[0:1, i, r * ROUND : r * ROUND + 1])
                regroup_g({1: 10, 2: 14}[r])
                for n in range(CHUNKS):
                    finish((r - 1) * CHUNKS + n)
        for n in range(CHUNKS):
            finish(SUBS - CHUNKS + n)
